import numpy as np
import ml_dtypes


def mxq(x, axis, fmt="e4m3"):
    dtype, down = {"e4m3": (ml_dtypes.float8_e4m3fn, 7), "e5m2": (ml_dtypes.float8_e5m2, 14)}[fmt]
    v = np.moveaxis(np.asarray(x, np.float32).astype(ml_dtypes.bfloat16).astype(np.float64), axis, -1)
    blocks = v.reshape(v.shape[:-1] + (-1, 32))
    amax = np.abs(blocks).max(-1, keepdims=True)
    byte = np.maximum(np.where(amax > 0, np.frexp(amax)[1] - 1 + 127, 0) - down, 1)
    scale = np.exp2(byte - 127.0)
    codes = (blocks / scale).astype(np.float32).astype(dtype).astype(np.float64)
    return np.moveaxis((codes * scale).reshape(v.shape), -1, axis)


WIDE = False


def mx_kscale(k):
    if not WIDE:
        return np.ones(k)
    levels = np.array([10, -10, 5, -5, 0])
    a = np.random.permutation(np.resize(levels, k // 512 * 4)).reshape(k // 512, 4)
    idx = np.arange(k)
    return np.exp2(a[idx // 512, idx % 128 // 32])


BF16 = ml_dtypes.bfloat16


def bf(x):
    return np.asarray(x, np.float32).astype(BF16)


def f64(x):
    return np.asarray(x).astype(np.float64)


B, CI, CO, H, WD = 2, 512, 128, 4, 16
NT = 12


def setup_inputs():
    s = mx_kscale(CI)
    inp = {f"x{i}": bf(np.random.standard_normal((B, CI, H, WD)) * s[None, :, None, None]) for i in range(NT)}
    inp["W"] = bf(np.random.standard_normal((CI, CO)) / np.sqrt(CI) / s[:, None])
    inp["b"] = bf(np.random.standard_normal(CO) * 0.1)
    return inp


def reference(x0, x1, x2, x3, x4, x5, x6, x7, x8, x9, x10, x11, W, b):
    xs = np.stack([f64(x0), f64(x1), f64(x2), f64(x3), f64(x4), f64(x5), f64(x6), f64(x7), f64(x8), f64(x9), f64(x10), f64(x11)])
    n, nb, ci, h, wd = xs.shape
    xq = mxq(xs, 2, "e4m3")
    wq = mxq(f64(W), 0, "e4m3")
    co = wq.shape[1]
    y = (wq.T @ xq.reshape(n, nb, ci, h * wd)).reshape(n, nb, co, h, wd)
    hout = NT * h
    out = np.transpose(y, (1, 2, 3, 0, 4)).reshape(nb, co, hout, wd)
    r = np.arange(hout)
    count = (np.minimum(NT - 1, r) - np.maximum(0, r - hout + NT) + 1).astype(np.float64)
    out = out + f64(b)[:, None, None] * count[None, :, None]
    return out

@@ -1,0 +1,128 @@
+import concourse.mybir as mybir
+
+BF16 = mybir.dt.bfloat16
+F32 = mybir.dt.float32
+I32 = mybir.dt.int32
+U32 = mybir.dt.uint32
+U8 = mybir.dt.uint8
+FP8X4 = mybir.dt.float8_e4m3fn_x4
+ALU = mybir.AluOpType
+
+P = 128
+PACK = 4
+MAPS = 12
+NB, CI, H, WD = 2, 512, 4, 16
+CO = 128
+PIXELS = H * WD
+MAP_COLS = NB * PIXELS
+ROWS = MAPS * H
+MAPS_PER_PASS = 2
+PASSES = MAPS // MAPS_PER_PASS
+PASS_COLS = MAPS_PER_PASS * MAP_COLS
+BANK_F32 = 512
+
+FLOPS = 2 * CI * CO * MAPS * MAP_COLS
+
+
+def tile_construct_s_kernel(
+    tc, x0, x1, x2, x3, x4, x5, x6, x7, x8, x9, x10, x11, W, b, out
+):
+    nc = tc.nc
+    maps = [x0, x1, x2, x3, x4, x5, x6, x7, x8, x9, x10, x11]
+
+    with tc.tile_pool(name="keep", bufs=1) as keep, tc.tile_pool(
+        name="stage", bufs=PASSES
+    ) as stage, tc.psum_pool(name="psum", bufs=PASSES) as psum:
+        w_raw = keep.tile([P, PACK, CO], BF16)
+        nc.scalar.dma_start(out=w_raw[:], in_=W.rearrange("(p j) o -> p j o", j=PACK))
+        b_col = keep.tile([P, 1], BF16)
+        nc.scalar.dma_start(out=b_col[:], in_=b.rearrange("(o u) -> o u", u=1))
+        x_raw = []
+        for i in range(MAPS):
+            raw = keep.tile([P, NB, PACK, PIXELS], BF16, name="x_raw%d" % i)
+            nc.sync.dma_start(
+                out=raw[:].rearrange("p n j q -> p n (j q)"),
+                in_=maps[i].rearrange("n (p j) h w -> p n (j h w)", j=PACK),
+            )
+            x_raw.append(raw)
+
+        row_int = keep.tile([P, NB, ROWS], I32)
+        nc.gpsimd.iota(row_int[:], pattern=[[0, NB], [1, ROWS]], base=0, channel_multiplier=0)
+        row = keep.tile([P, NB, ROWS], F32)
+        nc.vector.tensor_copy(out=row[:], in_=row_int[:])
+        rising = keep.tile([P, NB, ROWS], F32)
+        nc.vector.tensor_scalar(
+            out=rising[:], in0=row[:], scalar1=float(MAPS - 1), scalar2=1.0,
+            op0=ALU.min, op1=ALU.add,
+        )
+        falling = keep.tile([P, NB, ROWS], F32)
+        nc.vector.tensor_scalar(
+            out=falling[:], in0=row[:], scalar1=float(ROWS - MAPS), scalar2=0.0,
+            op0=ALU.subtract, op1=ALU.max,
+        )
+        count = keep.tile([P, NB, ROWS], F32)
+        nc.vector.tensor_tensor(out=count[:], in0=rising[:], in1=falling[:], op=ALU.subtract)
+        b_f32 = keep.tile([P, 1], F32)
+        nc.vector.tensor_copy(out=b_f32[:], in_=b_col[:])
+        bias = keep.tile([P, NB, H, MAPS], F32)
+        nc.vector.tensor_scalar_mul(
+            out=bias[:].rearrange("p n h i -> p n (h i)"), in0=count[:], scalar1=b_f32[:, 0:1]
+        )
+
+        w_grouped = keep.tile([P, CO, PACK], BF16, align_bytes=64)
+        nc.vector.tensor_copy(out=w_grouped[:], in_=w_raw[:].rearrange("p j o -> p o j"))
+        w_codes = keep.tile([P, CO], U32, align_bytes=64)
+        w_scales = keep.tile([P, CO], U8, align_bytes=64)
+        nc.vector.quantize_mx(
+            out=w_codes[:].bitcast(FP8X4),
+            scales=w_scales[:],
+            in_=w_grouped[:].rearrange("p o j -> p (o j)"),
+        )
+
+        out_sb = keep.tile([P, NB, H, MAPS, WD], F32)
+        for c in range(PASSES):
+            first = c * MAPS_PER_PASS
+            grouped = stage.tile([P, PASS_COLS, PACK], BF16, align_bytes=64)
+            for t in range(MAPS_PER_PASS):
+                dst = grouped[:, t * MAP_COLS : (t + 1) * MAP_COLS, :].rearrange(
+                    "p (n q) j -> p n q j", n=NB
+                )
+                src = x_raw[first + t][:].rearrange("p n j q -> p n q j")
+                if (first + t) % 2 == 0:
+                    nc.scalar.copy(out=dst, in_=src)
+                else:
+                    nc.vector.tensor_copy(out=dst, in_=src)
+            codes = stage.tile([P, PASS_COLS], U32, align_bytes=64)
+            scales = stage.tile([P, PASS_COLS], U8, align_bytes=64)
+            nc.vector.quantize_mx(
+                out=codes[:].bitcast(FP8X4),
+                scales=scales[:],
+                in_=grouped[:].rearrange("p c j -> p (c j)"),
+            )
+            acc = psum.tile([P, BANK_F32], F32)
+            nc.tensor.matmul_mx(
+                out=acc[:, :PASS_COLS],
+                lhsT=w_codes[:].bitcast(FP8X4),
+                lhsT_scale=w_scales[:],
+                rhs=codes[:].bitcast(FP8X4),
+                rhs_scale=scales[:],
+                start=True,
+                stop=True,
+            )
+            these = slice(first, first + MAPS_PER_PASS)
+            nc.vector.tensor_tensor(
+                out=out_sb[:, :, :, these, :].rearrange("p n h t w -> p t (n h) w"),
+                in0=acc[:, :PASS_COLS].rearrange(
+                    "p (t g w) -> p t g w", t=MAPS_PER_PASS, w=WD
+                ),
+                in1=bias[:, :, :, these]
+                .rearrange("p n h t -> p t (n h)")
+                .unsqueeze(3)
+                .to_broadcast([P, MAPS_PER_PASS, NB * H, WD]),
+                op=ALU.add,
+            )
+
+        nc.sync.dma_start(
+            out=out.rearrange("n o r w -> o n (r w)"),
+            in_=out_sb[:].rearrange("p n h i w -> p n (h i w)"),
+        )

@@ -19,6 +19,7 @@ ROWS = MAPS * H
 MAPS_PER_PASS = 2
 PASSES = MAPS // MAPS_PER_PASS
 PASS_COLS = MAPS_PER_PASS * MAP_COLS
+VECTOR_EVERY = 3
 BANK_F32 = 512
 
 FLOPS = 2 * CI * CO * MAPS * MAP_COLS
@@ -30,9 +31,10 @@ def tile_construct_s_kernel(
     nc = tc.nc
     maps = [x0, x1, x2, x3, x4, x5, x6, x7, x8, x9, x10, x11]
 
-    with tc.tile_pool(name="keep", bufs=1) as keep, tc.tile_pool(
-        name="stage", bufs=PASSES
-    ) as stage, tc.psum_pool(name="psum", bufs=PASSES) as psum:
+    with tc.tile_pool(name="keep", bufs=1) as keep, tc.psum_pool(
+        name="psum", bufs=1
+    ) as psum, tc.manual_schedule():
+
         w_raw = keep.tile([P, PACK, CO], BF16)
         nc.scalar.dma_start(out=w_raw[:], in_=W.rearrange("(p j) o -> p j o", j=PACK))
         b_col = keep.tile([P, 1], BF16)
@@ -62,15 +64,15 @@ def tile_construct_s_kernel(
         )
         count = keep.tile([P, NB, ROWS], F32)
         nc.vector.tensor_tensor(out=count[:], in0=rising[:], in1=falling[:], op=ALU.subtract)
+
+        w_grouped = keep.tile([P, CO, PACK], BF16, align_bytes=64)
+        nc.vector.tensor_copy(out=w_grouped[:], in_=w_raw[:].rearrange("p j o -> p o j"))
         b_f32 = keep.tile([P, 1], F32)
         nc.vector.tensor_copy(out=b_f32[:], in_=b_col[:])
         bias = keep.tile([P, NB, H, MAPS], F32)
         nc.vector.tensor_scalar_mul(
             out=bias[:].rearrange("p n h i -> p n (h i)"), in0=count[:], scalar1=b_f32[:, 0:1]
         )
-
-        w_grouped = keep.tile([P, CO, PACK], BF16, align_bytes=64)
-        nc.vector.tensor_copy(out=w_grouped[:], in_=w_raw[:].rearrange("p j o -> p o j"))
         w_codes = keep.tile([P, CO], U32, align_bytes=64)
         w_scales = keep.tile([P, CO], U8, align_bytes=64)
         nc.vector.quantize_mx(
@@ -80,39 +82,48 @@ def tile_construct_s_kernel(
         )
 
         out_sb = keep.tile([P, NB, H, MAPS, WD], F32)
+        grouped, codes, scales, acc = [], [], [], []
         for c in range(PASSES):
-            first = c * MAPS_PER_PASS
-            grouped = stage.tile([P, PASS_COLS, PACK], BF16, align_bytes=64)
+            grouped.append(
+                keep.tile([P, PASS_COLS, PACK], BF16, align_bytes=64, name="grouped%d" % c)
+            )
+            codes.append(keep.tile([P, PASS_COLS], U32, align_bytes=64, name="codes%d" % c))
+            scales.append(keep.tile([P, PASS_COLS], U8, align_bytes=64, name="scales%d" % c))
+            acc.append(psum.tile([P, BANK_F32], F32, name="acc%d" % c))
+
+        def regroup(c):
             for t in range(MAPS_PER_PASS):
-                dst = grouped[:, t * MAP_COLS : (t + 1) * MAP_COLS, :].rearrange(
+                i = c * MAPS_PER_PASS + t
+                dst = grouped[c][:, t * MAP_COLS : (t + 1) * MAP_COLS, :].rearrange(
                     "p (n q) j -> p n q j", n=NB
                 )
-                src = x_raw[first + t][:].rearrange("p n j q -> p n q j")
-                if (first + t) % 2 == 0:
-                    nc.scalar.copy(out=dst, in_=src)
-                else:
+                src = x_raw[i][:].rearrange("p n j q -> p n q j")
+                if i % VECTOR_EVERY == VECTOR_EVERY - 1:
                     nc.vector.tensor_copy(out=dst, in_=src)
-            codes = stage.tile([P, PASS_COLS], U32, align_bytes=64)
-            scales = stage.tile([P, PASS_COLS], U8, align_bytes=64)
+                else:
+                    nc.scalar.copy(out=dst, in_=src)
+
+        def quantise_and_multiply(c):
             nc.vector.quantize_mx(
-                out=codes[:].bitcast(FP8X4),
-                scales=scales[:],
-                in_=grouped[:].rearrange("p c j -> p (c j)"),
+                out=codes[c][:].bitcast(FP8X4),
+                scales=scales[c][:],
+                in_=grouped[c][:].rearrange("p c j -> p (c j)"),
             )
-            acc = psum.tile([P, BANK_F32], F32)
             nc.tensor.matmul_mx(
-                out=acc[:, :PASS_COLS],
+                out=acc[c][:, :PASS_COLS],
                 lhsT=w_codes[:].bitcast(FP8X4),
                 lhsT_scale=w_scales[:],
-                rhs=codes[:].bitcast(FP8X4),
-                rhs_scale=scales[:],
+                rhs=codes[c][:].bitcast(FP8X4),
+                rhs_scale=scales[c][:],
                 start=True,
                 stop=True,
             )
-            these = slice(first, first + MAPS_PER_PASS)
+
+        def add_bias(c):
+            these = slice(c * MAPS_PER_PASS, (c + 1) * MAPS_PER_PASS)
             nc.vector.tensor_tensor(
                 out=out_sb[:, :, :, these, :].rearrange("p n h t w -> p t (n h) w"),
-                in0=acc[:, :PASS_COLS].rearrange(
+                in0=acc[c][:, :PASS_COLS].rearrange(
                     "p (t g w) -> p t g w", t=MAPS_PER_PASS, w=WD
                 ),
                 in1=bias[:, :, :, these]
@@ -121,6 +132,15 @@ def tile_construct_s_kernel(
                 .to_broadcast([P, MAPS_PER_PASS, NB * H, WD]),
                 op=ALU.add,
             )
+
+        regroup(0)
+        for c in range(PASSES + 1):
+            if c + 1 < PASSES:
+                regroup(c + 1)
+            if c < PASSES:
+                quantise_and_multiply(c)
+            if c >= 1:
+                add_bias(c - 1)
 
         nc.sync.dma_start(
             out=out.rearrange("n o r w -> o n (r w)"),

@@ -20,6 +20,7 @@ MAPS_PER_PASS = 2
 PASSES = MAPS // MAPS_PER_PASS
 PASS_COLS = MAPS_PER_PASS * MAP_COLS
 VECTOR_EVERY = 3
+RUN = 4
 BANK_F32 = 512
 
 FLOPS = 2 * CI * CO * MAPS * MAP_COLS
@@ -66,7 +67,10 @@ def tile_construct_s_kernel(
         nc.vector.tensor_tensor(out=count[:], in0=rising[:], in1=falling[:], op=ALU.subtract)
 
         w_grouped = keep.tile([P, CO, PACK], BF16, align_bytes=64)
-        nc.vector.tensor_copy(out=w_grouped[:], in_=w_raw[:].rearrange("p j o -> p o j"))
+        nc.vector.tensor_copy(
+            out=w_grouped[:].rearrange("p (s r) j -> p s j r", r=RUN),
+            in_=w_raw[:].rearrange("p j (s r) -> p s j r", r=RUN),
+        )
         b_f32 = keep.tile([P, 1], F32)
         nc.vector.tensor_copy(out=b_f32[:], in_=b_col[:])
         bias = keep.tile([P, NB, H, MAPS], F32)
@@ -95,9 +99,9 @@ def tile_construct_s_kernel(
             for t in range(MAPS_PER_PASS):
                 i = c * MAPS_PER_PASS + t
                 dst = grouped[c][:, t * MAP_COLS : (t + 1) * MAP_COLS, :].rearrange(
-                    "p (n q) j -> p n q j", n=NB
+                    "p (n s r) j -> p n s j r", n=NB, r=RUN
                 )
-                src = x_raw[i][:].rearrange("p n j q -> p n q j")
+                src = x_raw[i][:].rearrange("p n j (s r) -> p n s j r", r=RUN)
                 if i % VECTOR_EVERY == VECTOR_EVERY - 1:
                     nc.vector.tensor_copy(out=dst, in_=src)
                 else:

@@ -21,6 +21,7 @@ PASSES = MAPS // MAPS_PER_PASS
 PASS_COLS = MAPS_PER_PASS * MAP_COLS
 VECTOR_EVERY = 3
 RUN = 4
+STORE_MAPS = 4
 BANK_F32 = 512
 
 FLOPS = 2 * CI * CO * MAPS * MAP_COLS
@@ -85,7 +86,9 @@ def tile_construct_s_kernel(
             in_=w_grouped[:].rearrange("p o j -> p (o j)"),
         )
 
-        out_sb = keep.tile([P, NB, H, MAPS, WD], F32)
+        out_sb = []
+        for g in range(MAPS // STORE_MAPS):
+            out_sb.append(keep.tile([P, NB, H, STORE_MAPS, WD], F32, name="out_sb%d" % g))
         grouped, codes, scales, acc = [], [], [], []
         for c in range(PASSES):
             grouped.append(
@@ -124,9 +127,13 @@ def tile_construct_s_kernel(
             )
 
         def add_bias(c):
-            these = slice(c * MAPS_PER_PASS, (c + 1) * MAPS_PER_PASS)
+            first = c * MAPS_PER_PASS
+            these = slice(first, first + MAPS_PER_PASS)
+            place = slice(first % STORE_MAPS, first % STORE_MAPS + MAPS_PER_PASS)
             nc.vector.tensor_tensor(
-                out=out_sb[:, :, :, these, :].rearrange("p n h t w -> p t (n h) w"),
+                out=out_sb[first // STORE_MAPS][:, :, :, place, :].rearrange(
+                    "p n h t w -> p t (n h) w"
+                ),
                 in0=acc[c][:, :PASS_COLS].rearrange(
                     "p (t g w) -> p t g w", t=MAPS_PER_PASS, w=WD
                 ),
@@ -137,16 +144,21 @@ def tile_construct_s_kernel(
                 op=ALU.add,
             )
 
+        def store(g):
+            these = slice(g * STORE_MAPS, (g + 1) * STORE_MAPS)
+            for n in range(NB):
+                nc.sync.dma_start(
+                    out=out[n].rearrange("o (h i) w -> o h i w", i=MAPS)[:, :, these, :],
+                    in_=out_sb[g][:, n],
+                )
+
         regroup(0)
         for c in range(PASSES + 1):
-            if c + 1 < PASSES:
-                regroup(c + 1)
             if c < PASSES:
                 quantise_and_multiply(c)
+            if c + 1 < PASSES:
+                regroup(c + 1)
             if c >= 1:
                 add_bias(c - 1)
-
-        nc.sync.dma_start(
-            out=out.rearrange("n o r w -> o n (r w)"),
-            in_=out_sb[:].rearrange("p n h i w -> p n (h i w)"),
-        )
+                if (c * MAPS_PER_PASS) % STORE_MAPS == 0:
+                    store(c * MAPS_PER_PASS // STORE_MAPS - 1)

@@ -19,7 +19,7 @@ ROWS = MAPS * H
 MAPS_PER_PASS = 2
 PASSES = MAPS // MAPS_PER_PASS
 PASS_COLS = MAPS_PER_PASS * MAP_COLS
-VECTOR_EVERY = 3
+VECTOR_MAPS = (3, 7, 11)
 RUN = 4
 STORE_MAPS = 4
 BANK_F32 = 512
@@ -105,7 +105,7 @@ def tile_construct_s_kernel(
                     "p (n s r) j -> p n s j r", n=NB, r=RUN
                 )
                 src = x_raw[i][:].rearrange("p n j (s r) -> p n s j r", r=RUN)
-                if i % VECTOR_EVERY == VECTOR_EVERY - 1:
+                if i in VECTOR_MAPS:
                     nc.vector.tensor_copy(out=dst, in_=src)
                 else:
                     nc.scalar.copy(out=dst, in_=src)

@@ -19,7 +19,10 @@ ROWS = MAPS * H
 MAPS_PER_PASS = 2
 PASSES = MAPS // MAPS_PER_PASS
 PASS_COLS = MAPS_PER_PASS * MAP_COLS
-VECTOR_MAPS = (3, 7, 11)
+UNITS = PASSES * MAPS_PER_PASS
+VECTOR_UNITS = (3, 7, 11)
+WHOLE_MAPS = 8
+WHOLE_PASSES = WHOLE_MAPS // MAPS_PER_PASS
 RUN = 4
 STORE_MAPS = 4
 BANK_F32 = 512
@@ -42,13 +45,22 @@ def tile_construct_s_kernel(
         b_col = keep.tile([P, 1], BF16)
         nc.scalar.dma_start(out=b_col[:], in_=b.rearrange("(o u) -> o u", u=1))
         x_raw = []
-        for i in range(MAPS):
+        for i in range(WHOLE_MAPS):
             raw = keep.tile([P, NB, PACK, PIXELS], BF16, name="x_raw%d" % i)
             nc.sync.dma_start(
                 out=raw[:].rearrange("p n j q -> p n (j q)"),
                 in_=maps[i].rearrange("n (p j) h w -> p n (j h w)", j=PACK),
             )
             x_raw.append(raw)
+        for n in range(NB):
+            for first in range(WHOLE_MAPS, MAPS, 2):
+                raw = keep.tile([P, 2, PACK, PIXELS], BF16, name="x_raw%d_%d" % (first, n))
+                for m in range(2):
+                    nc.sync.dma_start(
+                        out=raw[:, m].rearrange("p j q -> p (j q)"),
+                        in_=maps[first + m][n].rearrange("(p j) h w -> p (j h w)", j=PACK),
+                    )
+                x_raw.append(raw)
 
         row_int = keep.tile([P, NB, ROWS], I32)
         nc.gpsimd.iota(row_int[:], pattern=[[0, NB], [1, ROWS]], base=0, channel_multiplier=0)
@@ -105,7 +117,7 @@ def tile_construct_s_kernel(
                     "p (n s r) j -> p n s j r", n=NB, r=RUN
                 )
                 src = x_raw[i][:].rearrange("p n j (s r) -> p n s j r", r=RUN)
-                if i in VECTOR_MAPS:
+                if i in VECTOR_UNITS:
                     nc.vector.tensor_copy(out=dst, in_=src)
                 else:
                     nc.scalar.copy(out=dst, in_=src)
@@ -126,7 +138,27 @@ def tile_construct_s_kernel(
                 stop=True,
             )
 
+        def add_bias_last(n):
+            nc.vector.tensor_tensor(
+                out=out_sb[WHOLE_MAPS // STORE_MAPS][:, n].rearrange("p h t w -> p t h w"),
+                in0=acc[WHOLE_PASSES + n][:, :PASS_COLS].rearrange(
+                    "p (t h w) -> p t h w", h=H, w=WD
+                ),
+                in1=bias[:, n, :, WHOLE_MAPS:]
+                .rearrange("p h t -> p t h")
+                .unsqueeze(3)
+                .to_broadcast([P, MAPS - WHOLE_MAPS, H, WD]),
+                op=ALU.add,
+            )
+            nc.sync.dma_start(
+                out=out[n].rearrange("o (h i) w -> o h i w", i=MAPS)[:, :, WHOLE_MAPS:, :],
+                in_=out_sb[WHOLE_MAPS // STORE_MAPS][:, n],
+            )
+
         def add_bias(c):
+            if c >= WHOLE_PASSES:
+                add_bias_last(c - WHOLE_PASSES)
+                return
             first = c * MAPS_PER_PASS
             these = slice(first, first + MAPS_PER_PASS)
             place = slice(first % STORE_MAPS, first % STORE_MAPS + MAPS_PER_PASS)
@@ -160,5 +192,5 @@ def tile_construct_s_kernel(
                 regroup(c + 1)
             if c >= 1:
                 add_bias(c - 1)
-                if (c * MAPS_PER_PASS) % STORE_MAPS == 0:
+                if (c * MAPS_PER_PASS) % STORE_MAPS == 0 and c <= WHOLE_PASSES:
                     store(c * MAPS_PER_PASS // STORE_MAPS - 1)

@@ -14,20 +14,18 @@ MAPS = 12
 NB, CI, H, WD = 2, 512, 4, 16
 CO = 128
 PIXELS = H * WD
-MAP_COLS = NB * PIXELS
+UNIT_COLS = NB * PIXELS
 ROWS = MAPS * H
-MAPS_PER_PASS = 2
-PASSES = MAPS // MAPS_PER_PASS
-PASS_COLS = MAPS_PER_PASS * MAP_COLS
-UNITS = PASSES * MAPS_PER_PASS
-VECTOR_UNITS = (3, 7, 11)
 WHOLE_MAPS = 8
-WHOLE_PASSES = WHOLE_MAPS // MAPS_PER_PASS
+LAST_MAPS = MAPS - WHOLE_MAPS
+PASS_UNITS = ((0, 1), (2, 3), (4, 5), (6, 7), (8, 9), (10, 11))
+VECTOR_UNITS = (1, 5, 9)
+STORE_GROUPS = ((0, 4), (4, 4))
+ORDER = "W0 c0 c1 B0 Q0 q0 c2 c3 q1 c4 c5 a0 q2 c6 c7 a1 s0 q3 c8 c9 a2 q4 c10 c11 a3 s1 q5 a4 t0 a5 t1".split()
 RUN = 4
-STORE_MAPS = 4
 BANK_F32 = 512
 
-FLOPS = 2 * CI * CO * MAPS * MAP_COLS
+FLOPS = 2 * CI * CO * MAPS * NB * PIXELS
 
 
 def tile_construct_s_kernel(
@@ -80,56 +78,65 @@ def tile_construct_s_kernel(
         nc.vector.tensor_tensor(out=count[:], in0=rising[:], in1=falling[:], op=ALU.subtract)
 
         w_grouped = keep.tile([P, CO, PACK], BF16, align_bytes=64)
-        nc.vector.tensor_copy(
-            out=w_grouped[:].rearrange("p (s r) j -> p s j r", r=RUN),
-            in_=w_raw[:].rearrange("p j (s r) -> p s j r", r=RUN),
-        )
         b_f32 = keep.tile([P, 1], F32)
-        nc.vector.tensor_copy(out=b_f32[:], in_=b_col[:])
         bias = keep.tile([P, NB, H, MAPS], F32)
-        nc.vector.tensor_scalar_mul(
-            out=bias[:].rearrange("p n h i -> p n (h i)"), in0=count[:], scalar1=b_f32[:, 0:1]
-        )
         w_codes = keep.tile([P, CO], U32, align_bytes=64)
         w_scales = keep.tile([P, CO], U8, align_bytes=64)
-        nc.vector.quantize_mx(
-            out=w_codes[:].bitcast(FP8X4),
-            scales=w_scales[:],
-            in_=w_grouped[:].rearrange("p o j -> p (o j)"),
-        )
+
+        def regroup_weight():
+            nc.vector.tensor_copy(
+                out=w_grouped[:].rearrange("p (s r) j -> p s j r", r=RUN),
+                in_=w_raw[:].rearrange("p j (s r) -> p s j r", r=RUN),
+            )
+
+        def make_bias():
+            nc.vector.tensor_copy(out=b_f32[:], in_=b_col[:])
+            nc.vector.tensor_scalar_mul(
+                out=bias[:].rearrange("p n h i -> p n (h i)"), in0=count[:], scalar1=b_f32[:, 0:1]
+            )
+
+        def quantise_weight():
+            nc.vector.quantize_mx(
+                out=w_codes[:].bitcast(FP8X4),
+                scales=w_scales[:],
+                in_=w_grouped[:].rearrange("p o j -> p (o j)"),
+            )
 
         out_sb = []
-        for g in range(MAPS // STORE_MAPS):
-            out_sb.append(keep.tile([P, NB, H, STORE_MAPS, WD], F32, name="out_sb%d" % g))
-        grouped, codes, scales, acc = [], [], [], []
-        for c in range(PASSES):
-            grouped.append(
-                keep.tile([P, PASS_COLS, PACK], BF16, align_bytes=64, name="grouped%d" % c)
+        for g in range(len(STORE_GROUPS)):
+            out_sb.append(
+                keep.tile([P, NB, H, STORE_GROUPS[g][1], WD], F32, name="out_sb%d" % g)
             )
-            codes.append(keep.tile([P, PASS_COLS], U32, align_bytes=64, name="codes%d" % c))
-            scales.append(keep.tile([P, PASS_COLS], U8, align_bytes=64, name="scales%d" % c))
+        out_last = keep.tile([P, NB, H, LAST_MAPS, WD], F32)
+        grouped, codes, scales, acc = [], [], [], []
+        for c in range(len(PASS_UNITS)):
+            cols = len(PASS_UNITS[c]) * UNIT_COLS
+            grouped.append(keep.tile([P, cols, PACK], BF16, align_bytes=64, name="grouped%d" % c))
+            codes.append(keep.tile([P, cols], U32, align_bytes=64, name="codes%d" % c))
+            scales.append(keep.tile([P, cols], U8, align_bytes=64, name="scales%d" % c))
             acc.append(psum.tile([P, BANK_F32], F32, name="acc%d" % c))
 
-        def regroup(c):
-            for t in range(MAPS_PER_PASS):
-                i = c * MAPS_PER_PASS + t
-                dst = grouped[c][:, t * MAP_COLS : (t + 1) * MAP_COLS, :].rearrange(
-                    "p (n s r) j -> p n s j r", n=NB, r=RUN
-                )
-                src = x_raw[i][:].rearrange("p n j (s r) -> p n s j r", r=RUN)
-                if i in VECTOR_UNITS:
-                    nc.vector.tensor_copy(out=dst, in_=src)
-                else:
-                    nc.scalar.copy(out=dst, in_=src)
+        def regroup(u):
+            c = [k for k in range(len(PASS_UNITS)) if u in PASS_UNITS[k]][0]
+            t = PASS_UNITS[c].index(u)
+            dst = grouped[c][:, t * UNIT_COLS : (t + 1) * UNIT_COLS, :].rearrange(
+                "p (n s r) j -> p n s j r", n=NB, r=RUN
+            )
+            src = x_raw[u][:].rearrange("p n j (s r) -> p n s j r", r=RUN)
+            if u in VECTOR_UNITS:
+                nc.vector.tensor_copy(out=dst, in_=src)
+            else:
+                nc.scalar.copy(out=dst, in_=src)
 
         def quantise_and_multiply(c):
+            cols = len(PASS_UNITS[c]) * UNIT_COLS
             nc.vector.quantize_mx(
                 out=codes[c][:].bitcast(FP8X4),
                 scales=scales[c][:],
                 in_=grouped[c][:].rearrange("p c j -> p (c j)"),
             )
             nc.tensor.matmul_mx(
-                out=acc[c][:, :PASS_COLS],
+                out=acc[c][:, :cols],
                 lhsT=w_codes[:].bitcast(FP8X4),
                 lhsT_scale=w_scales[:],
                 rhs=codes[c][:].bitcast(FP8X4),
@@ -138,59 +145,64 @@ def tile_construct_s_kernel(
                 stop=True,
             )
 
-        def add_bias_last(n):
-            nc.vector.tensor_tensor(
-                out=out_sb[WHOLE_MAPS // STORE_MAPS][:, n].rearrange("p h t w -> p t h w"),
-                in0=acc[WHOLE_PASSES + n][:, :PASS_COLS].rearrange(
-                    "p (t h w) -> p t h w", h=H, w=WD
-                ),
-                in1=bias[:, n, :, WHOLE_MAPS:]
-                .rearrange("p h t -> p t h")
-                .unsqueeze(3)
-                .to_broadcast([P, MAPS - WHOLE_MAPS, H, WD]),
-                op=ALU.add,
-            )
-            nc.sync.dma_start(
-                out=out[n].rearrange("o (h i) w -> o h i w", i=MAPS)[:, :, WHOLE_MAPS:, :],
-                in_=out_sb[WHOLE_MAPS // STORE_MAPS][:, n],
-            )
-
         def add_bias(c):
-            if c >= WHOLE_PASSES:
-                add_bias_last(c - WHOLE_PASSES)
-                return
-            first = c * MAPS_PER_PASS
-            these = slice(first, first + MAPS_PER_PASS)
-            place = slice(first % STORE_MAPS, first % STORE_MAPS + MAPS_PER_PASS)
-            nc.vector.tensor_tensor(
-                out=out_sb[first // STORE_MAPS][:, :, :, place, :].rearrange(
-                    "p n h t w -> p t (n h) w"
-                ),
-                in0=acc[c][:, :PASS_COLS].rearrange(
-                    "p (t g w) -> p t g w", t=MAPS_PER_PASS, w=WD
-                ),
-                in1=bias[:, :, :, these]
-                .rearrange("p n h t -> p t (n h)")
-                .unsqueeze(3)
-                .to_broadcast([P, MAPS_PER_PASS, NB * H, WD]),
-                op=ALU.add,
-            )
+            units = PASS_UNITS[c]
+            cols = len(units) * UNIT_COLS
+            if units[0] < WHOLE_MAPS:
+                first, many = units[0], len(units)
+                g = [k for k in range(len(STORE_GROUPS)) if STORE_GROUPS[k][0] <= first < STORE_GROUPS[k][0] + STORE_GROUPS[k][1]][0]
+                place = slice(first - STORE_GROUPS[g][0], first - STORE_GROUPS[g][0] + many)
+                nc.vector.tensor_tensor(
+                    out=out_sb[g][:, :, :, place, :].rearrange("p n h t w -> p t (n h) w"),
+                    in0=acc[c][:, :cols].rearrange("p (t g w) -> p t g w", t=many, w=WD),
+                    in1=bias[:, :, :, first : first + many]
+                    .rearrange("p n h t -> p t (n h)")
+                    .unsqueeze(3)
+                    .to_broadcast([P, many, NB * H, WD]),
+                    op=ALU.add,
+                )
+            else:
+                k = units[0] - WHOLE_MAPS
+                n, first, many = k // (LAST_MAPS // 2), 2 * (k % (LAST_MAPS // 2)), 2 * len(units)
+                nc.vector.tensor_tensor(
+                    out=out_last[:, n, :, first : first + many, :].rearrange("p h t w -> p t h w"),
+                    in0=acc[c][:, :cols].rearrange("p (t h w) -> p t h w", h=H, w=WD),
+                    in1=bias[:, n, :, WHOLE_MAPS + first : WHOLE_MAPS + first + many]
+                    .rearrange("p h t -> p t h")
+                    .unsqueeze(3)
+                    .to_broadcast([P, many, H, WD]),
+                    op=ALU.add,
+                )
 
         def store(g):
-            these = slice(g * STORE_MAPS, (g + 1) * STORE_MAPS)
+            these = slice(STORE_GROUPS[g][0], STORE_GROUPS[g][0] + STORE_GROUPS[g][1])
             for n in range(NB):
                 nc.sync.dma_start(
                     out=out[n].rearrange("o (h i) w -> o h i w", i=MAPS)[:, :, these, :],
                     in_=out_sb[g][:, n],
                 )
 
-        regroup(0)
-        for c in range(PASSES + 1):
-            if c < PASSES:
-                quantise_and_multiply(c)
-            if c + 1 < PASSES:
-                regroup(c + 1)
-            if c >= 1:
-                add_bias(c - 1)
-                if (c * MAPS_PER_PASS) % STORE_MAPS == 0 and c <= WHOLE_PASSES:
-                    store(c * MAPS_PER_PASS // STORE_MAPS - 1)
+        def store_last(n):
+            nc.sync.dma_start(
+                out=out[n].rearrange("o (h i) w -> o h i w", i=MAPS)[:, :, WHOLE_MAPS:, :],
+                in_=out_last[:, n],
+            )
+
+        for step in ORDER:
+            kind, k = step[0], int(step[1:])
+            if kind == "W":
+                regroup_weight()
+            elif kind == "B":
+                make_bias()
+            elif kind == "Q":
+                quantise_weight()
+            elif kind == "c":
+                regroup(k)
+            elif kind == "q":
+                quantise_and_multiply(k)
+            elif kind == "a":
+                add_bias(k)
+            elif kind == "s":
+                store(k)
+            elif kind == "t":
+                store_last(k)

@@ -22,7 +22,7 @@ PASS_UNITS = ((0, 1), (2, 3), (4, 5), (6, 7), (8, 9), (10, 11))
 VECTOR_UNITS = (1, 5, 9)
 STORE_GROUPS = ((0, 4), (4, 4))
 ORDER = "W0 c0 c1 B0 Q0 q0 c2 c3 q1 c4 c5 a0 q2 c6 c7 a1 s0 q3 c8 c9 a2 q4 c10 c11 a3 s1 q5 a4 t0 a5 t1".split()
-RUN = 4
+RUN = 8
 BANK_F32 = 512
 
 FLOPS = 2 * CI * CO * MAPS * NB * PIXELS

@@ -19,9 +19,11 @@ ROWS = MAPS * H
 WHOLE_MAPS = 8
 LAST_MAPS = MAPS - WHOLE_MAPS
 PASS_UNITS = ((0, 1), (2, 3), (4, 5), (6, 7), (8, 9), (10, 11))
-VECTOR_UNITS = (1, 5, 9)
+VECTOR_UNITS = (1, 5, 7, 9)
 STORE_GROUPS = ((0, 4), (4, 4))
-ORDER = "W0 c0 c1 B0 Q0 q0 c2 c3 q1 c4 c5 a0 q2 c6 c7 a1 s0 q3 c8 c9 a2 q4 c10 c11 a3 s1 q5 a4 t0 a5 t1".split()
+ORDER = "c0 c1 q0 W0 Q0 m0 c2 c3 q1 m1 B0 c4 c5 a0 q2 m2 c6 c7 a1 s0 q3 m3 c8 c9 a2 q4 m4 c10 c11 a3 s1 q5 m5 a4 t0 a5 t1".split()
+WEIGHT_AFTER = 2
+BIAS_AFTER = 3
 RUN = 8
 BANK_F32 = 512
 
@@ -39,9 +41,7 @@ def tile_construct_s_kernel(
     ) as psum, tc.manual_schedule():
 
         w_raw = keep.tile([P, PACK, CO], BF16)
-        nc.scalar.dma_start(out=w_raw[:], in_=W.rearrange("(p j) o -> p j o", j=PACK))
         b_col = keep.tile([P, 1], BF16)
-        nc.scalar.dma_start(out=b_col[:], in_=b.rearrange("(o u) -> o u", u=1))
         x_raw = []
         for i in range(WHOLE_MAPS):
             raw = keep.tile([P, NB, PACK, PIXELS], BF16, name="x_raw%d" % i)
@@ -50,6 +50,10 @@ def tile_construct_s_kernel(
                 in_=maps[i].rearrange("n (p j) h w -> p n (j h w)", j=PACK),
             )
             x_raw.append(raw)
+            if i == WEIGHT_AFTER:
+                nc.sync.dma_start(out=w_raw[:], in_=W.rearrange("(p j) o -> p j o", j=PACK))
+            if i == BIAS_AFTER:
+                nc.sync.dma_start(out=b_col[:], in_=b.rearrange("(o u) -> o u", u=1))
         for n in range(NB):
             for first in range(WHOLE_MAPS, MAPS, 2):
                 raw = keep.tile([P, 2, PACK, PIXELS], BF16, name="x_raw%d_%d" % (first, n))
@@ -128,13 +132,16 @@ def tile_construct_s_kernel(
             else:
                 nc.scalar.copy(out=dst, in_=src)
 
-        def quantise_and_multiply(c):
+        def quantise(c):
             cols = len(PASS_UNITS[c]) * UNIT_COLS
             nc.vector.quantize_mx(
                 out=codes[c][:].bitcast(FP8X4),
                 scales=scales[c][:],
                 in_=grouped[c][:].rearrange("p c j -> p (c j)"),
             )
+
+        def multiply(c):
+            cols = len(PASS_UNITS[c]) * UNIT_COLS
             nc.tensor.matmul_mx(
                 out=acc[c][:, :cols],
                 lhsT=w_codes[:].bitcast(FP8X4),
@@ -199,7 +206,9 @@ def tile_construct_s_kernel(
             elif kind == "c":
                 regroup(k)
             elif kind == "q":
-                quantise_and_multiply(k)
+                quantise(k)
+            elif kind == "m":
+                multiply(k)
             elif kind == "a":
                 add_bias(k)
             elif kind == "s":

@@ -2,7 +2,6 @@ import concourse.mybir as mybir
 
 BF16 = mybir.dt.bfloat16
 F32 = mybir.dt.float32
-I32 = mybir.dt.int32
 U32 = mybir.dt.uint32
 U8 = mybir.dt.uint8
 FP8X4 = mybir.dt.float8_e4m3fn_x4
@@ -15,7 +14,6 @@ NB, CI, H, WD = 2, 512, 4, 16
 CO = 128
 PIXELS = H * WD
 UNIT_COLS = NB * PIXELS
-ROWS = MAPS * H
 WHOLE_MAPS = 8
 LAST_MAPS = MAPS - WHOLE_MAPS
 PASS_UNITS = ((0, 1), (2, 3), (4, 5), (6, 7), (8, 9), (10, 11))
@@ -64,22 +62,19 @@ def tile_construct_s_kernel(
                     )
                 x_raw.append(raw)
 
-        row_int = keep.tile([P, NB, ROWS], I32)
-        nc.gpsimd.iota(row_int[:], pattern=[[0, NB], [1, ROWS]], base=0, channel_multiplier=0)
-        row = keep.tile([P, NB, ROWS], F32)
-        nc.vector.tensor_copy(out=row[:], in_=row_int[:])
-        rising = keep.tile([P, NB, ROWS], F32)
+        count = keep.tile([P, NB, H, MAPS], F32)
+        ones = keep.tile([P, NB * MAPS], F32)
+        nc.vector.memset(ones[:], 1.0)
+        nc.vector.memset(count[:, :, 1:3, :], float(MAPS))
+        for n in range(NB):
+            nc.vector.tensor_tensor_scan(
+                out=count[:, n, 0, :], data0=ones[:, :MAPS], data1=ones[:, :MAPS], initial=0.0,
+                op0=ALU.mult, op1=ALU.add,
+            )
         nc.vector.tensor_scalar(
-            out=rising[:], in0=row[:], scalar1=float(MAPS - 1), scalar2=1.0,
-            op0=ALU.min, op1=ALU.add,
+            out=count[:, :, 3, :], in0=count[:, :, 0, :], scalar1=-1.0, scalar2=float(MAPS + 1),
+            op0=ALU.mult, op1=ALU.add,
         )
-        falling = keep.tile([P, NB, ROWS], F32)
-        nc.vector.tensor_scalar(
-            out=falling[:], in0=row[:], scalar1=float(ROWS - MAPS), scalar2=0.0,
-            op0=ALU.subtract, op1=ALU.max,
-        )
-        count = keep.tile([P, NB, ROWS], F32)
-        nc.vector.tensor_tensor(out=count[:], in0=rising[:], in1=falling[:], op=ALU.subtract)
 
         w_grouped = keep.tile([P, CO, PACK], BF16, align_bytes=64)
         b_f32 = keep.tile([P, 1], F32)
@@ -96,7 +91,7 @@ def tile_construct_s_kernel(
         def make_bias():
             nc.vector.tensor_copy(out=b_f32[:], in_=b_col[:])
             nc.vector.tensor_scalar_mul(
-                out=bias[:].rearrange("p n h i -> p n (h i)"), in0=count[:], scalar1=b_f32[:, 0:1]
+                out=bias[:].rearrange("p n h i -> p n (h i)"), in0=count[:].rearrange("p n h i -> p n (h i)"), scalar1=b_f32[:, 0:1]
             )
 
         def quantise_weight():

@@ -17,9 +17,10 @@ UNIT_COLS = NB * PIXELS
 WHOLE_MAPS = 8
 LAST_MAPS = MAPS - WHOLE_MAPS
 PASS_UNITS = ((0, 1), (2, 3), (4, 5), (6, 7), (8, 9), (10, 11))
-VECTOR_UNITS = (1, 5, 7, 9)
+VECTOR_UNITS = (1, 4, 7, 10)
 STORE_GROUPS = ((0, 4), (4, 4))
-ORDER = "c0 c1 q0 W0 Q0 m0 c2 c3 q1 m1 B0 c4 c5 a0 q2 m2 c6 c7 a1 s0 q3 m3 c8 c9 a2 q4 m4 c10 c11 a3 s1 q5 m5 a4 t0 a5 t1".split()
+ORDER = "c0 c1 q0 W0 Q0 m0 c2 c3 q1 m1 B0 c4 c5 a0 q2 m2 c6 c7 a1 s0 q3 m3 c8 c9 a2 c10 q4 m4 c11 a3 s1 q5 m5 a4 t0 a5 t1".split()
+SPLIT_UNIT = 11
 WEIGHT_AFTER = 2
 BIAS_AFTER = 3
 RUN = 8
@@ -118,14 +119,18 @@ def tile_construct_s_kernel(
         def regroup(u):
             c = [k for k in range(len(PASS_UNITS)) if u in PASS_UNITS[k]][0]
             t = PASS_UNITS[c].index(u)
-            dst = grouped[c][:, t * UNIT_COLS : (t + 1) * UNIT_COLS, :].rearrange(
-                "p (n s r) j -> p n s j r", n=NB, r=RUN
-            )
-            src = x_raw[u][:].rearrange("p n j (s r) -> p n s j r", r=RUN)
-            if u in VECTOR_UNITS:
-                nc.vector.tensor_copy(out=dst, in_=src)
-            else:
-                nc.scalar.copy(out=dst, in_=src)
+            for part in (range(NB) if u == SPLIT_UNIT else (slice(0, NB),)):
+                part = part if u != SPLIT_UNIT else slice(part, part + 1)
+                halves = part.stop - part.start
+                first = t * UNIT_COLS + part.start * PIXELS
+                dst = grouped[c][:, first : first + halves * PIXELS, :].rearrange(
+                    "p (n s r) j -> p n s j r", n=halves, r=RUN
+                )
+                src = x_raw[u][:, part].rearrange("p n j (s r) -> p n s j r", r=RUN)
+                if u in VECTOR_UNITS:
+                    nc.vector.tensor_copy(out=dst, in_=src)
+                else:
+                    nc.scalar.copy(out=dst, in_=src)
 
         def quantise(c):
             cols = len(PASS_UNITS[c]) * UNIT_COLS

@@ -13,16 +13,17 @@ MAPS = 12
 NB, CI, H, WD = 2, 512, 4, 16
 CO = 128
 PIXELS = H * WD
+ROWS = MAPS * H
 UNIT_COLS = NB * PIXELS
 WHOLE_MAPS = 8
 LAST_MAPS = MAPS - WHOLE_MAPS
 PASS_UNITS = ((0, 1), (2, 3), (4, 5), (6, 7), (8, 9), (10, 11))
 VECTOR_UNITS = (1, 4, 7, 10)
 STORE_GROUPS = ((0, 4), (4, 4))
-ORDER = "c0 c1 q0 W0 Q0 m0 c2 c3 q1 m1 B0 c4 c5 a0 q2 m2 c6 c7 a1 s0 q3 m3 c8 c9 a2 c10 q4 m4 c11 a3 s1 q5 m5 a4 t0 a5 t1".split()
+ORDER = "c0 c1 q0 W0 B0 D0 Q0 m0 c2 c3 q1 m1 c4 c5 a0 q2 m2 c6 c7 a1 s0 q3 m3 c8 c9 a2 c10 q4 m4 c11 a3 s1 q5 m5 a4 t0 a5 t1".split()
 SPLIT_UNIT = 11
 WEIGHT_AFTER = 2
-BIAS_AFTER = 3
+BIAS_AFTER = 2
 RUN = 8
 BANK_F32 = 512
 
@@ -40,7 +41,8 @@ def tile_construct_s_kernel(
     ) as psum, tc.manual_schedule():
 
         w_raw = keep.tile([P, PACK, CO], BF16)
-        b_col = keep.tile([P, 1], BF16)
+        b_rows = keep.tile([P, CO], BF16)
+        nc.vector.memset(b_rows[:], 0.0)
         x_raw = []
         for i in range(WHOLE_MAPS):
             raw = keep.tile([P, NB, PACK, PIXELS], BF16, name="x_raw%d" % i)
@@ -52,7 +54,7 @@ def tile_construct_s_kernel(
             if i == WEIGHT_AFTER:
                 nc.sync.dma_start(out=w_raw[:], in_=W.rearrange("(p j) o -> p j o", j=PACK))
             if i == BIAS_AFTER:
-                nc.sync.dma_start(out=b_col[:], in_=b.rearrange("(o u) -> o u", u=1))
+                nc.sync.dma_start(out=b_rows[0:1, :], in_=b.rearrange("(u o) -> u o", u=1))
         for n in range(NB):
             for first in range(WHOLE_MAPS, MAPS, 2):
                 raw = keep.tile([P, 2, PACK, PIXELS], BF16, name="x_raw%d_%d" % (first, n))
@@ -63,7 +65,7 @@ def tile_construct_s_kernel(
                     )
                 x_raw.append(raw)
 
-        count = keep.tile([P, NB, H, MAPS], F32)
+        count = keep.tile([P, NB, H, MAPS], BF16)
         ones = keep.tile([P, NB * MAPS], F32)
         nc.vector.memset(ones[:], 1.0)
         nc.vector.memset(count[:, :, 1:3, :], float(MAPS))
@@ -78,7 +80,7 @@ def tile_construct_s_kernel(
         )
 
         w_grouped = keep.tile([P, CO, PACK], BF16, align_bytes=64)
-        b_f32 = keep.tile([P, 1], F32)
+        acc_bias = psum.tile([P, BANK_F32], F32)
         bias = keep.tile([P, NB, H, MAPS], F32)
         w_codes = keep.tile([P, CO], U32, align_bytes=64)
         w_scales = keep.tile([P, CO], U8, align_bytes=64)
@@ -90,10 +92,16 @@ def tile_construct_s_kernel(
             )
 
         def make_bias():
-            nc.vector.tensor_copy(out=b_f32[:], in_=b_col[:])
-            nc.vector.tensor_scalar_mul(
-                out=bias[:].rearrange("p n h i -> p n (h i)"), in0=count[:].rearrange("p n h i -> p n (h i)"), scalar1=b_f32[:, 0:1]
+            nc.tensor.matmul(
+                out=acc_bias[:, : NB * ROWS],
+                lhsT=b_rows[:],
+                rhs=count[:].rearrange("p n h i -> p (n h i)"),
+                start=True,
+                stop=True,
             )
+
+        def copy_bias():
+            nc.vector.tensor_copy(out=bias[:].rearrange("p n h i -> p (n h i)"), in_=acc_bias[:, : NB * ROWS])
 
         def quantise_weight():
             nc.vector.quantize_mx(
@@ -201,6 +209,8 @@ def tile_construct_s_kernel(
                 regroup_weight()
             elif kind == "B":
                 make_bias()
+            elif kind == "D":
+                copy_bias()
             elif kind == "Q":
                 quantise_weight()
             elif kind == "c":

@@ -24,6 +24,7 @@ ORDER = "c0 c1 q0 W0 B0 D0 Q0 m0 c2 c3 q1 m1 c4 c5 a0 q2 m2 c6 c7 a1 s0 q3 m3 c8
 SPLIT_UNIT = 11
 WEIGHT_AFTER = 2
 BIAS_AFTER = 2
+DMA_ALIGN = 256
 RUN = 8
 BANK_F32 = 512
 
@@ -40,12 +41,12 @@ def tile_construct_s_kernel(
         name="psum", bufs=1
     ) as psum, tc.manual_schedule():
 
-        w_raw = keep.tile([P, PACK, CO], BF16)
-        b_rows = keep.tile([P, CO], BF16)
+        w_raw = keep.tile([P, PACK, CO], BF16, align_bytes=DMA_ALIGN)
+        b_rows = keep.tile([P, CO], BF16, align_bytes=DMA_ALIGN)
         nc.vector.memset(b_rows[:], 0.0)
         x_raw = []
         for i in range(WHOLE_MAPS):
-            raw = keep.tile([P, NB, PACK, PIXELS], BF16, name="x_raw%d" % i)
+            raw = keep.tile([P, NB, PACK, PIXELS], BF16, align_bytes=DMA_ALIGN, name="x_raw%d" % i)
             nc.sync.dma_start(
                 out=raw[:].rearrange("p n j q -> p n (j q)"),
                 in_=maps[i].rearrange("n (p j) h w -> p n (j h w)", j=PACK),
@@ -57,7 +58,7 @@ def tile_construct_s_kernel(
                 nc.sync.dma_start(out=b_rows[0:1, :], in_=b.rearrange("(u o) -> u o", u=1))
         for n in range(NB):
             for first in range(WHOLE_MAPS, MAPS, 2):
-                raw = keep.tile([P, 2, PACK, PIXELS], BF16, name="x_raw%d_%d" % (first, n))
+                raw = keep.tile([P, 2, PACK, PIXELS], BF16, align_bytes=DMA_ALIGN, name="x_raw%d_%d" % (first, n))
                 for m in range(2):
                     nc.sync.dma_start(
                         out=raw[:, m].rearrange("p j q -> p (j q)"),
@@ -113,9 +114,9 @@ def tile_construct_s_kernel(
         out_sb = []
         for g in range(len(STORE_GROUPS)):
             out_sb.append(
-                keep.tile([P, NB, H, STORE_GROUPS[g][1], WD], F32, name="out_sb%d" % g)
+                keep.tile([P, NB, H, STORE_GROUPS[g][1], WD], F32, align_bytes=DMA_ALIGN, name="out_sb%d" % g)
             )
-        out_last = keep.tile([P, NB, H, LAST_MAPS, WD], F32)
+        out_last = keep.tile([P, NB, H, LAST_MAPS, WD], F32, align_bytes=DMA_ALIGN)
         grouped, codes, scales, acc = [], [], [], []
         for c in range(len(PASS_UNITS)):
             cols = len(PASS_UNITS[c]) * UNIT_COLS

@@ -18,13 +18,13 @@ UNIT_COLS = NB * PIXELS
 WHOLE_MAPS = 8
 LAST_MAPS = MAPS - WHOLE_MAPS
 PASS_UNITS = ((0, 1), (2, 3), (4, 5), (6, 7), (8, 9), (10, 11))
-VECTOR_UNITS = (1, 4, 7, 10)
+VECTOR_UNITS = (0, 1, 4, 7, 10)
 STORE_GROUPS = ((0, 4), (4, 4))
 ORDER = "c0 c1 q0 W0 B0 D0 Q0 m0 c2 c3 q1 m1 c4 c5 a0 q2 m2 c6 c7 a1 s0 q3 m3 c8 c9 a2 c10 q4 m4 c11 a3 s1 q5 m5 a4 t0 a5 t1".split()
 SPLIT_UNIT = 11
 WEIGHT_AFTER = 2
 BIAS_AFTER = 2
-DMA_ALIGN = 256
+DMA_ALIGN = 1024
 RUN = 8
 BANK_F32 = 512
 

import concourse.mybir as mybir

BF16 = mybir.dt.bfloat16
F32 = mybir.dt.float32
U32 = mybir.dt.uint32
U8 = mybir.dt.uint8
FP8X4 = mybir.dt.float8_e4m3fn_x4
ALU = mybir.AluOpType

P = 128
PACK = 4
MAPS = 12
NB, CI, H, WD = 2, 512, 4, 16
CO = 128
PIXELS = H * WD
ROWS = MAPS * H
UNIT_COLS = NB * PIXELS
WHOLE_MAPS = 8
LAST_MAPS = MAPS - WHOLE_MAPS
PASS_UNITS = ((0, 1), (2, 3), (4, 5), (6, 7), (8, 9), (10, 11))
VECTOR_UNITS = (0, 1, 4, 7, 10)
STORE_GROUPS = ((0, 4), (4, 4))
ORDER = "c0 c1 q0 W0 B0 D0 Q0 m0 c2 c3 q1 m1 c4 c5 a0 q2 m2 c6 c7 a1 s0 q3 m3 c8 c9 a2 c10 q4 m4 c11 a3 s1 q5 m5 a4 t0 a5 t1".split()
SPLIT_UNIT = 11
WEIGHT_AFTER = 2
BIAS_AFTER = 2
DMA_ALIGN = 1024
RUN = 8
BANK_F32 = 512

FLOPS = 2 * CI * CO * MAPS * NB * PIXELS


def tile_construct_s_kernel(
    tc, x0, x1, x2, x3, x4, x5, x6, x7, x8, x9, x10, x11, W, b, out
):
    nc = tc.nc
    maps = [x0, x1, x2, x3, x4, x5, x6, x7, x8, x9, x10, x11]

    with tc.tile_pool(name="keep", bufs=1) as keep, tc.psum_pool(
        name="psum", bufs=1
    ) as psum, tc.manual_schedule():

        w_raw = keep.tile([P, PACK, CO], BF16, align_bytes=DMA_ALIGN)
        b_rows = keep.tile([P, CO], BF16, align_bytes=DMA_ALIGN)
        nc.vector.memset(b_rows[:], 0.0)
        x_raw = []
        for i in range(WHOLE_MAPS):
            raw = keep.tile([P, NB, PACK, PIXELS], BF16, align_bytes=DMA_ALIGN, name="x_raw%d" % i)
            nc.sync.dma_start(
                out=raw[:].rearrange("p n j q -> p n (j q)"),
                in_=maps[i].rearrange("n (p j) h w -> p n (j h w)", j=PACK),
            )
            x_raw.append(raw)
            if i == WEIGHT_AFTER:
                nc.sync.dma_start(out=w_raw[:], in_=W.rearrange("(p j) o -> p j o", j=PACK))
            if i == BIAS_AFTER:
                nc.sync.dma_start(out=b_rows[0:1, :], in_=b.rearrange("(u o) -> u o", u=1))
        for n in range(NB):
            for first in range(WHOLE_MAPS, MAPS, 2):
                raw = keep.tile([P, 2, PACK, PIXELS], BF16, align_bytes=DMA_ALIGN, name="x_raw%d_%d" % (first, n))
                for m in range(2):
                    nc.sync.dma_start(
                        out=raw[:, m].rearrange("p j q -> p (j q)"),
                        in_=maps[first + m][n].rearrange("(p j) h w -> p (j h w)", j=PACK),
                    )
                x_raw.append(raw)

        count = keep.tile([P, NB, H, MAPS], BF16)
        ones = keep.tile([P, NB * MAPS], F32)
        nc.vector.memset(ones[:], 1.0)
        nc.vector.memset(count[:, :, 1:3, :], float(MAPS))
        for n in range(NB):
            nc.vector.tensor_tensor_scan(
                out=count[:, n, 0, :], data0=ones[:, :MAPS], data1=ones[:, :MAPS], initial=0.0,
                op0=ALU.mult, op1=ALU.add,
            )
        nc.vector.tensor_scalar(
            out=count[:, :, 3, :], in0=count[:, :, 0, :], scalar1=-1.0, scalar2=float(MAPS + 1),
            op0=ALU.mult, op1=ALU.add,
        )

        w_grouped = keep.tile([P, CO, PACK], BF16, align_bytes=64)
        acc_bias = psum.tile([P, BANK_F32], F32)
        bias = keep.tile([P, NB, H, MAPS], F32)
        w_codes = keep.tile([P, CO], U32, align_bytes=64)
        w_scales = keep.tile([P, CO], U8, align_bytes=64)

        def regroup_weight():
            nc.vector.tensor_copy(
                out=w_grouped[:].rearrange("p (s r) j -> p s j r", r=RUN),
                in_=w_raw[:].rearrange("p j (s r) -> p s j r", r=RUN),
            )

        def make_bias():
            nc.tensor.matmul(
                out=acc_bias[:, : NB * ROWS],
                lhsT=b_rows[:],
                rhs=count[:].rearrange("p n h i -> p (n h i)"),
                start=True,
                stop=True,
            )

        def copy_bias():
            nc.vector.tensor_copy(out=bias[:].rearrange("p n h i -> p (n h i)"), in_=acc_bias[:, : NB * ROWS])

        def quantise_weight():
            nc.vector.quantize_mx(
                out=w_codes[:].bitcast(FP8X4),
                scales=w_scales[:],
                in_=w_grouped[:].rearrange("p o j -> p (o j)"),
            )

        out_sb = []
        for g in range(len(STORE_GROUPS)):
            out_sb.append(
                keep.tile([P, NB, H, STORE_GROUPS[g][1], WD], F32, align_bytes=DMA_ALIGN, name="out_sb%d" % g)
            )
        out_last = keep.tile([P, NB, H, LAST_MAPS, WD], F32, align_bytes=DMA_ALIGN)
        grouped, codes, scales, acc = [], [], [], []
        for c in range(len(PASS_UNITS)):
            cols = len(PASS_UNITS[c]) * UNIT_COLS
            grouped.append(keep.tile([P, cols, PACK], BF16, align_bytes=64, name="grouped%d" % c))
            codes.append(keep.tile([P, cols], U32, align_bytes=64, name="codes%d" % c))
            scales.append(keep.tile([P, cols], U8, align_bytes=64, name="scales%d" % c))
            acc.append(psum.tile([P, BANK_F32], F32, name="acc%d" % c))

        def regroup(u):
            c = [k for k in range(len(PASS_UNITS)) if u in PASS_UNITS[k]][0]
            t = PASS_UNITS[c].index(u)
            for part in (range(NB) if u == SPLIT_UNIT else (slice(0, NB),)):
                part = part if u != SPLIT_UNIT else slice(part, part + 1)
                halves = part.stop - part.start
                first = t * UNIT_COLS + part.start * PIXELS
                dst = grouped[c][:, first : first + halves * PIXELS, :].rearrange(
                    "p (n s r) j -> p n s j r", n=halves, r=RUN
                )
                src = x_raw[u][:, part].rearrange("p n j (s r) -> p n s j r", r=RUN)
                if u in VECTOR_UNITS:
                    nc.vector.tensor_copy(out=dst, in_=src)
                else:
                    nc.scalar.copy(out=dst, in_=src)

        def quantise(c):
            cols = len(PASS_UNITS[c]) * UNIT_COLS
            nc.vector.quantize_mx(
                out=codes[c][:].bitcast(FP8X4),
                scales=scales[c][:],
                in_=grouped[c][:].rearrange("p c j -> p (c j)"),
            )

        def multiply(c):
            cols = len(PASS_UNITS[c]) * UNIT_COLS
            nc.tensor.matmul_mx(
                out=acc[c][:, :cols],
                lhsT=w_codes[:].bitcast(FP8X4),
                lhsT_scale=w_scales[:],
                rhs=codes[c][:].bitcast(FP8X4),
                rhs_scale=scales[c][:],
                start=True,
                stop=True,
            )

        def add_bias(c):
            units = PASS_UNITS[c]
            cols = len(units) * UNIT_COLS
            if units[0] < WHOLE_MAPS:
                first, many = units[0], len(units)
                g = [k for k in range(len(STORE_GROUPS)) if STORE_GROUPS[k][0] <= first < STORE_GROUPS[k][0] + STORE_GROUPS[k][1]][0]
                place = slice(first - STORE_GROUPS[g][0], first - STORE_GROUPS[g][0] + many)
                nc.vector.tensor_tensor(
                    out=out_sb[g][:, :, :, place, :].rearrange("p n h t w -> p t (n h) w"),
                    in0=acc[c][:, :cols].rearrange("p (t g w) -> p t g w", t=many, w=WD),
                    in1=bias[:, :, :, first : first + many]
                    .rearrange("p n h t -> p t (n h)")
                    .unsqueeze(3)
                    .to_broadcast([P, many, NB * H, WD]),
                    op=ALU.add,
                )
            else:
                k = units[0] - WHOLE_MAPS
                n, first, many = k // (LAST_MAPS // 2), 2 * (k % (LAST_MAPS // 2)), 2 * len(units)
                nc.vector.tensor_tensor(
                    out=out_last[:, n, :, first : first + many, :].rearrange("p h t w -> p t h w"),
                    in0=acc[c][:, :cols].rearrange("p (t h w) -> p t h w", h=H, w=WD),
                    in1=bias[:, n, :, WHOLE_MAPS + first : WHOLE_MAPS + first + many]
                    .rearrange("p h t -> p t h")
                    .unsqueeze(3)
                    .to_broadcast([P, many, H, WD]),
                    op=ALU.add,
                )

        def store(g):
            these = slice(STORE_GROUPS[g][0], STORE_GROUPS[g][0] + STORE_GROUPS[g][1])
            for n in range(NB):
                nc.sync.dma_start(
                    out=out[n].rearrange("o (h i) w -> o h i w", i=MAPS)[:, :, these, :],
                    in_=out_sb[g][:, n],
                )

        def store_last(n):
            nc.sync.dma_start(
                out=out[n].rearrange("o (h i) w -> o h i w", i=MAPS)[:, :, WHOLE_MAPS:, :],
                in_=out_last[:, n],
            )

        for step in ORDER:
            kind, k = step[0], int(step[1:])
            if kind == "W":
                regroup_weight()
            elif kind == "B":
                make_bias()
            elif kind == "D":
                copy_bias()
            elif kind == "Q":
                quantise_weight()
            elif kind == "c":
                regroup(k)
            elif kind == "q":
                quantise(k)
            elif kind == "m":
                multiply(k)
            elif kind == "a":
                add_bias(k)
            elif kind == "s":
                store(k)
            elif kind == "t":
                store_last(k)
